import numpy as np
import ml_dtypes


def mxq(x, axis, fmt="e4m3"):
    dtype, down = {"e4m3": (ml_dtypes.float8_e4m3fn, 7), "e5m2": (ml_dtypes.float8_e5m2, 14)}[fmt]
    v = np.moveaxis(np.asarray(x, np.float32).astype(ml_dtypes.bfloat16).astype(np.float64), axis, -1)
    blocks = v.reshape(v.shape[:-1] + (-1, 32))
    amax = np.abs(blocks).max(-1, keepdims=True)
    byte = np.maximum(np.where(amax > 0, np.frexp(amax)[1] - 1 + 127, 0) - down, 1)
    scale = np.exp2(byte - 127.0)
    codes = (blocks / scale).astype(np.float32).astype(dtype).astype(np.float64)
    return np.moveaxis((codes * scale).reshape(v.shape), -1, axis)


WIDE = False


def mx_kscale(k):
    if not WIDE:
        return np.ones(k)
    levels = np.array([10, -10, 5, -5, 0])
    a = np.random.permutation(np.resize(levels, k // 512 * 4)).reshape(k // 512, 4)
    idx = np.arange(k)
    return np.exp2(a[idx // 512, idx % 128 // 32])


BF16 = ml_dtypes.bfloat16


def bf(x):
    return np.asarray(x, np.float32).astype(BF16)


def f64(x):
    return np.asarray(x).astype(np.float64)


B, S, H, NH, FF = 8, 512, 512, 4, 3072
HD = H // NH
EPS = 1e-7


def layer_norm(x, g, b):
    m = x.mean(-1, keepdims=True)
    v = ((x - m) ** 2).mean(-1, keepdims=True)
    return (x - m) / np.sqrt(v + EPS) * g + b


def heads(t):
    return t.reshape(B, S, NH, HD).transpose(0, 2, 1, 3)


def setup_inputs():
    s = mx_kscale(H)
    r = np.random.standard_normal
    return {"x": bf(r((B, S, H))), "pos_emb": bf(r((S, H)) * 0.5),
            "emb_ln_g": bf((1.0 + 0.1 * r(H)) * s), "emb_ln_b": bf(0.1 * r(H) * s),
            "Wq": bf(r((H, H)) * 1.5 / np.sqrt(H) / s[:, None]),
            "Wk": bf(r((H, H)) * 1.5 / np.sqrt(H) / s[:, None]),
            "Wv": bf(r((H, H)) * 2.0 / np.sqrt(H) / s[:, None]),
            "q_bias": bf(r(H) * 0.3), "v_bias": bf(r(H) * 0.3)}


def reference(x, pos_emb, emb_ln_g, emb_ln_b, Wq, Wk, Wv, q_bias, v_bias):
    h = layer_norm(f64(x) + f64(pos_emb), f64(emb_ln_g), f64(emb_ln_b))
    hq = mxq(h, 2, "e4m3")
    q = heads((hq @ mxq(f64(Wq), 0, "e4m3")) + f64(q_bias))
    k = heads(hq @ mxq(f64(Wk), 0, "e4m3"))
    v = heads((hq @ mxq(f64(Wv), 0, "e4m3")) + f64(v_bias))
    return q / np.sqrt(HD), k, v

@@ -1,0 +1,254 @@
+from contextlib import ExitStack
+import math
+
+import concourse.mybir as mybir
+from concourse.masks import make_identity
+
+F32 = mybir.dt.float32
+BF16 = mybir.dt.bfloat16
+U32 = mybir.dt.uint32
+U8 = mybir.dt.uint8
+FP8X4 = mybir.dt.float8_e4m3fn_x4
+ALU = mybir.AluOpType
+ACT = mybir.ActivationFunctionType
+
+P = 128
+PACK = 4
+B, S, H, NH, HD = 8, 512, 512, 4, 128
+ROW_TILES = S // P
+EPS = 1e-7
+Q_SCALE = 1.0 / math.sqrt(HD)
+
+FLOPS = 2 * B * S * H * 3 * H
+
+
+def tile_disentangledattention_pa_t_kernel(
+    tc, x, pos_emb, emb_ln_g, emb_ln_b, Wq, Wk, Wv, q_bias, v_bias, out_0, out_1, out_2
+):
+    nc = tc.nc
+    with ExitStack() as ctx:
+        ctx.enter_context(tc.manual_schedule())
+        const = ctx.enter_context(tc.tile_pool(name="const", bufs=1))
+        xs = ctx.enter_context(tc.tile_pool(name="xs", bufs=B))
+        work = ctx.enter_context(tc.tile_pool(name="work", bufs=2))
+        small = ctx.enter_context(tc.tile_pool(name="small", bufs=3))
+        outs = ctx.enter_context(tc.tile_pool(name="outs", bufs=3))
+        psum_t = ctx.enter_context(tc.psum_pool(name="psum_t", bufs=1))
+        psum_acc = ctx.enter_context(tc.psum_pool(name="psum_acc", bufs=4))
+
+        x_sb, u, mean_var, std, neg_mean, rstd, z, h_t, h_codes, h_scales = (
+            {}, {}, {}, {}, {}, {}, {}, {}, {}, {},
+        )
+
+        def load_x(b):
+            x_sb[b] = xs.tile([P, ROW_TILES, H], BF16, name="x_b")
+            nc.sync.dma_start(out=x_sb[b][:], in_=x[b].rearrange("(p j) h -> p j h", j=ROW_TILES))
+
+        def regroup(engine_copy, dst, src):
+            engine_copy(
+                out=dst.rearrange("p (c i) t -> p c t i", i=4),
+                in_=src.rearrange("p t (c i) -> p c t i", i=4),
+            )
+
+        def add_pos(engine, b):
+            u[b] = work.tile([P, ROW_TILES, H], F32, name="u")
+            engine.tensor_tensor(out=u[b][:], in0=x_sb[b][:], in1=pos_sb[:], op=ALU.add)
+
+        def row_stats(b):
+            stats = small.tile([P, ROW_TILES, 6], F32, name="stats")
+            mean_var[b] = small.tile([P, ROW_TILES, 2], F32, name="mean_var")
+            for j in range(ROW_TILES):
+                nc.vector.bn_stats(out=stats[:, j, :], in_=u[b][:, j, :])
+                nc.vector.bn_aggr(out=mean_var[b][:, j, :], in_=stats[:, j, :])
+
+        def row_std(b):
+            std[b] = small.tile([P, ROW_TILES], F32, name="std")
+            nc.scalar.activation(
+                out=std[b][:], in_=mean_var[b][:, :, 1], func=ACT.Sqrt, bias=EPS, scale=1.0
+            )
+
+        def row_factors(b):
+            rstd[b] = small.tile([P, ROW_TILES], F32, name="rstd")
+            nc.vector.reciprocal(out=rstd[b][:], in_=std[b][:])
+            neg_mean[b] = small.tile([P, ROW_TILES], F32, name="neg_mean")
+            nc.vector.tensor_scalar_mul(out=neg_mean[b][:], in0=mean_var[b][:, :, 0], scalar1=-1.0)
+
+        def normalise(engine, b):
+            z[b] = work.tile([P, ROW_TILES, H], F32, name="z")
+            for j in range(ROW_TILES):
+                engine.tensor_scalar(
+                    out=z[b][:, j, :],
+                    in0=u[b][:, j, :],
+                    scalar1=neg_mean[b][:, j : j + 1],
+                    scalar2=rstd[b][:, j : j + 1],
+                    op0=ALU.add,
+                    op1=ALU.mult,
+                )
+
+        def transpose(b):
+            banks = []
+            for t in range(PACK):
+                bank = psum_t.tile([P, S], F32, name="z_t%d" % t)
+                banks.append(bank)
+            for j in range(ROW_TILES):
+                for t in range(PACK):
+                    nc.tensor.transpose(
+                        banks[t][:, j * P : (j + 1) * P], z[b][:, j, t * P : (t + 1) * P], ident_f32[:]
+                    )
+            h_t[b] = work.tile([P, PACK, S], BF16, name="h_t")
+            return banks
+
+        def gain_bias(b, banks, t):
+            nc.scalar.activation(
+                out=h_t[b][:, t, :],
+                in_=banks[t][:],
+                func=ACT.Identity,
+                scale=gb_col[:, t : t + 1],
+                bias=gb_col[:, PACK + t : PACK + t + 1],
+            )
+
+        def quantise_h(b):
+            grouped = work.tile([P, S, PACK], BF16, name="grouped", align_bytes=64)
+            regroup(nc.scalar.copy, grouped[:], h_t[b][:])
+            h_codes[b] = work.tile([P, S], U32, name="h_codes", align_bytes=64)
+            h_scales[b] = work.tile([P, S], U8, name="h_scales", align_bytes=64)
+            nc.vector.quantize_mx(
+                out=h_codes[b][:].bitcast(FP8X4),
+                scales=h_scales[b][:],
+                in_=grouped[:].rearrange("p r t -> p (r t)"),
+            )
+
+        def project(b, j, o_q, o_k, o_v):
+            rows = slice(j * P, (j + 1) * P)
+            accs = []
+            for i in range(3):
+                acc = psum_acc.tile([P, H], F32, name="acc", tag="acc")
+                nc.tensor.matmul_mx(
+                    out=acc[:],
+                    lhsT=h_codes[b][:, rows].bitcast(FP8X4),
+                    lhsT_scale=h_scales[b][:, rows],
+                    rhs=w_codes[i][:].bitcast(FP8X4),
+                    rhs_scale=w_scales[i][:],
+                    start=True,
+                    stop=True,
+                )
+                accs.append(acc[:].rearrange("p (n d) -> p n d", n=NH))
+            nc.vector.scalar_tensor_tensor(
+                out=o_q[:, :, j, :],
+                in0=accs[0],
+                scalar=Q_SCALE,
+                in1=qb_scaled[:].rearrange("p (n d) -> p n d", n=NH),
+                op0=ALU.mult,
+                op1=ALU.add,
+            )
+            nc.scalar.copy(out=o_k[:, :, j, :], in_=accs[1])
+            nc.vector.tensor_tensor(
+                out=o_v[:, :, j, :],
+                in0=accs[2],
+                in1=vb_bc[:].rearrange("p (n d) -> p n d", n=NH),
+                op=ALU.add,
+            )
+
+        def store(b, o_sb, o_dram):
+            nc.sync.dma_start(
+                out=o_dram[b].rearrange("n (p j) d -> p n (j d)", j=ROW_TILES),
+                in_=o_sb[:].rearrange("p n j d -> p n (j d)"),
+            )
+
+        load_x(0)
+        pos_sb = const.tile([P, ROW_TILES, H], BF16)
+        nc.sync.dma_start(out=pos_sb[:], in_=pos_emb.rearrange("(p j) h -> p j h", j=ROW_TILES))
+        gb_rows = const.tile([P, P], BF16)
+        nc.vector.memset(gb_rows[:], 0.0)
+        nc.sync.dma_start(out=gb_rows[0:PACK, :], in_=emb_ln_g.rearrange("(t p) -> t p", p=P))
+        nc.sync.dma_start(out=gb_rows[PACK : 2 * PACK, :], in_=emb_ln_b.rearrange("(t p) -> t p", p=P))
+        load_x(1)
+        w_raw = []
+        for i, w in enumerate((Wq, Wk, Wv)):
+            raw = const.tile([P, PACK, H], BF16, name="w_raw%d" % i)
+            nc.sync.dma_start(out=raw[:], in_=w.rearrange("(t p) n -> p t n", p=P))
+            w_raw.append(raw)
+        load_x(2)
+        qb_bc = const.tile([P, H], BF16)
+        nc.sync.dma_start(out=qb_bc[:], in_=q_bias.partition_broadcast(P))
+        vb_bc = const.tile([P, H], BF16)
+        nc.sync.dma_start(out=vb_bc[:], in_=v_bias.partition_broadcast(P))
+        for b in range(3, B):
+            load_x(b)
+
+        ident_f32 = const.tile([P, P], F32)
+        make_identity(nc, ident_f32[:])
+        ident_bf16 = const.tile([P, P], BF16)
+        make_identity(nc, ident_bf16[:])
+        one = const.tile([P, 1], F32)
+        nc.vector.memset(one[:], 1.0)
+        warm = const.tile([P, 1], F32)
+        nc.scalar.activation(out=warm[:], in_=one[:], func=ACT.Sqrt)
+
+        grouped_w = []
+        for i in range(3):
+            g_w = const.tile([P, H, PACK], BF16, name="grouped_w%d" % i, align_bytes=64)
+            grouped_w.append(g_w)
+        add_pos(nc.vector, 0)
+        add_pos(nc.gpsimd, 1)
+        add_pos(nc.gpsimd, 2)
+        row_stats(0)
+        regroup(nc.scalar.copy, grouped_w[0][:], w_raw[0][:])
+        row_std(0)
+        gb_t = psum_acc.tile([P, P], BF16, tag="acc")
+        nc.tensor.transpose(gb_t[:], gb_rows[:], ident_bf16[:])
+        gb_col = const.tile([P, 2 * PACK], F32)
+        nc.vector.tensor_copy(out=gb_col[:], in_=gb_t[:, 0 : 2 * PACK])
+        row_factors(0)
+        normalise(nc.vector, 0)
+        banks = transpose(0)
+        regroup(nc.scalar.copy, grouped_w[1][:], w_raw[1][:])
+        regroup(nc.scalar.copy, grouped_w[2][:], w_raw[2][:])
+        row_stats(1)
+        row_std(1)
+        row_factors(1)
+        normalise(nc.gpsimd, 1)
+        row_stats(2)
+        w_codes = []
+        w_scales = []
+        for i in range(3):
+            codes = const.tile([P, H], U32, name="w_codes%d" % i, align_bytes=64)
+            scales = const.tile([P, H], U8, name="w_scales%d" % i, align_bytes=64)
+            nc.vector.quantize_mx(
+                out=codes[:].bitcast(FP8X4),
+                scales=scales[:],
+                in_=grouped_w[i][:].rearrange("p n t -> p (n t)"),
+            )
+            w_codes.append(codes)
+            w_scales.append(scales)
+        qb_scaled = const.tile([P, H], F32)
+        nc.vector.tensor_scalar_mul(out=qb_scaled[:], in0=qb_bc[:], scalar1=Q_SCALE)
+        for t in range(PACK):
+            gain_bias(0, banks, t)
+        quantise_h(0)
+
+        for b in range(B):
+            if b + 2 < B:
+                row_std(b + 2)
+            if b + 3 < B:
+                add_pos(nc.gpsimd, b + 3)
+            if b + 1 < B:
+                banks = transpose(b + 1)
+            o_q = outs.tile([P, NH, ROW_TILES, HD], F32, name="o_q")
+            o_k = outs.tile([P, NH, ROW_TILES, HD], F32, name="o_k")
+            o_v = outs.tile([P, NH, ROW_TILES, HD], F32, name="o_v")
+            for j in range(ROW_TILES):
+                if b + 1 < B:
+                    gain_bias(b + 1, banks, j)
+                project(b, j, o_q, o_k, o_v)
+                if j == 0 and b + 2 < B:
+                    row_factors(b + 2)
+            if b + 2 < B:
+                normalise(nc.gpsimd, b + 2)
+            store(b, o_q, out_0)
+            store(b, o_k, out_1)
+            store(b, o_v, out_2)
+            if b + 3 < B:
+                row_stats(b + 3)
+            if b + 1 < B:
+                quantise_h(b + 1)

@@ -19,6 +19,8 @@ ROW_TILES = S // P
 EPS = 1e-7
 Q_SCALE = 1.0 / math.sqrt(HD)
 
+Q, K, V = 0, 1, 2
+
 FLOPS = 2 * B * S * H * 3 * H
 
 
@@ -36,30 +38,34 @@ def tile_disentangledattention_pa_t_kernel(
         psum_t = ctx.enter_context(tc.psum_pool(name="psum_t", bufs=1))
         psum_acc = ctx.enter_context(tc.psum_pool(name="psum_acc", bufs=4))
 
-        x_sb, u, mean_var, std, neg_mean, rstd, z, h_t, h_codes, h_scales = (
-            {}, {}, {}, {}, {}, {}, {}, {}, {}, {},
-        )
+        x_sb, u, stats, mean_var, std, neg_mean, rstd = {}, {}, {}, {}, {}, {}, {}
+        z, z_t, h_t, grouped, h_codes, h_scales = {}, {}, {}, {}, {}, {}
+
+        def live(b):
+            return 0 <= b < B
 
         def load_x(b):
             x_sb[b] = xs.tile([P, ROW_TILES, H], BF16, name="x_b")
             nc.sync.dma_start(out=x_sb[b][:], in_=x[b].rearrange("(p j) h -> p j h", j=ROW_TILES))
 
-        def regroup(engine_copy, dst, src):
-            engine_copy(
+        def regroup(dst, src):
+            nc.scalar.copy(
                 out=dst.rearrange("p (c i) t -> p c t i", i=4),
                 in_=src.rearrange("p t (c i) -> p c t i", i=4),
             )
 
-        def add_pos(engine, b):
-            u[b] = work.tile([P, ROW_TILES, H], F32, name="u")
-            engine.tensor_tensor(out=u[b][:], in0=x_sb[b][:], in1=pos_sb[:], op=ALU.add)
+        def elementwise_engine(b):
+            return nc.vector if b == 0 else nc.gpsimd
 
-        def row_stats(b):
-            stats = small.tile([P, ROW_TILES, 6], F32, name="stats")
+        def add_pos(b):
+            u[b] = work.tile([P, ROW_TILES, H], F32, name="u", bufs=3)
+            elementwise_engine(b).tensor_tensor(out=u[b][:], in0=x_sb[b][:], in1=pos_sb[:], op=ALU.add)
+            stats[b] = small.tile([P, ROW_TILES, 6], F32, name="stats")
             mean_var[b] = small.tile([P, ROW_TILES, 2], F32, name="mean_var")
-            for j in range(ROW_TILES):
-                nc.vector.bn_stats(out=stats[:, j, :], in_=u[b][:, j, :])
-                nc.vector.bn_aggr(out=mean_var[b][:, j, :], in_=stats[:, j, :])
+
+        def row_stats(b, j):
+            nc.vector.bn_stats(out=stats[b][:, j, :], in_=u[b][:, j, :])
+            nc.vector.bn_aggr(out=mean_var[b][:, j, :], in_=stats[b][:, j, :])
 
         def row_std(b):
             std[b] = small.tile([P, ROW_TILES], F32, name="std")
@@ -73,10 +79,10 @@ def tile_disentangledattention_pa_t_kernel(
             neg_mean[b] = small.tile([P, ROW_TILES], F32, name="neg_mean")
             nc.vector.tensor_scalar_mul(out=neg_mean[b][:], in0=mean_var[b][:, :, 0], scalar1=-1.0)
 
-        def normalise(engine, b):
+        def normalise(b):
             z[b] = work.tile([P, ROW_TILES, H], F32, name="z")
             for j in range(ROW_TILES):
-                engine.tensor_scalar(
+                elementwise_engine(b).tensor_scalar(
                     out=z[b][:, j, :],
                     in0=u[b][:, j, :],
                     scalar1=neg_mean[b][:, j : j + 1],
@@ -86,68 +92,70 @@ def tile_disentangledattention_pa_t_kernel(
                 )
 
         def transpose(b):
-            banks = []
+            z_t[b] = []
             for t in range(PACK):
                 bank = psum_t.tile([P, S], F32, name="z_t%d" % t)
-                banks.append(bank)
+                z_t[b].append(bank)
             for j in range(ROW_TILES):
                 for t in range(PACK):
                     nc.tensor.transpose(
-                        banks[t][:, j * P : (j + 1) * P], z[b][:, j, t * P : (t + 1) * P], ident_f32[:]
+                        z_t[b][t][:, j * P : (j + 1) * P], z[b][:, j, t * P : (t + 1) * P], ident_f32[:]
                     )
             h_t[b] = work.tile([P, PACK, S], BF16, name="h_t")
-            return banks
 
-        def gain_bias(b, banks, t):
+        def gain_bias(b, t):
             nc.scalar.activation(
                 out=h_t[b][:, t, :],
-                in_=banks[t][:],
+                in_=z_t[b][t][:],
                 func=ACT.Identity,
                 scale=gb_col[:, t : t + 1],
                 bias=gb_col[:, PACK + t : PACK + t + 1],
             )
 
+        def regroup_h(b):
+            grouped[b] = work.tile([P, S, PACK], BF16, name="grouped", align_bytes=64)
+            regroup(grouped[b][:], h_t[b][:])
+
         def quantise_h(b):
-            grouped = work.tile([P, S, PACK], BF16, name="grouped", align_bytes=64)
-            regroup(nc.scalar.copy, grouped[:], h_t[b][:])
             h_codes[b] = work.tile([P, S], U32, name="h_codes", align_bytes=64)
             h_scales[b] = work.tile([P, S], U8, name="h_scales", align_bytes=64)
             nc.vector.quantize_mx(
                 out=h_codes[b][:].bitcast(FP8X4),
                 scales=h_scales[b][:],
-                in_=grouped[:].rearrange("p r t -> p (r t)"),
+                in_=grouped[b][:].rearrange("p r t -> p (r t)"),
             )
 
-        def project(b, j, o_q, o_k, o_v):
+        def project(b, i, j, o_sb):
             rows = slice(j * P, (j + 1) * P)
-            accs = []
-            for i in range(3):
-                acc = psum_acc.tile([P, H], F32, name="acc", tag="acc")
-                nc.tensor.matmul_mx(
-                    out=acc[:],
-                    lhsT=h_codes[b][:, rows].bitcast(FP8X4),
-                    lhsT_scale=h_scales[b][:, rows],
-                    rhs=w_codes[i][:].bitcast(FP8X4),
-                    rhs_scale=w_scales[i][:],
-                    start=True,
-                    stop=True,
+            acc = psum_acc.tile([P, H], F32, name="acc", tag="acc")
+            nc.tensor.matmul_mx(
+                out=acc[:],
+                lhsT=h_codes[b][:, rows].bitcast(FP8X4),
+                lhsT_scale=h_scales[b][:, rows],
+                rhs=w_codes[i][:].bitcast(FP8X4),
+                rhs_scale=w_scales[i][:],
+                start=True,
+                stop=True,
+            )
+            by_head = acc[:].rearrange("p (n d) -> p n d", n=NH)
+            if i == Q:
+                nc.vector.scalar_tensor_tensor(
+                    out=o_sb[:, :, j, :],
+                    in0=by_head,
+                    scalar=Q_SCALE,
+                    in1=qb_scaled[:].rearrange("p (n d) -> p n d", n=NH),
+                    op0=ALU.mult,
+                    op1=ALU.add,
                 )
-                accs.append(acc[:].rearrange("p (n d) -> p n d", n=NH))
-            nc.vector.scalar_tensor_tensor(
-                out=o_q[:, :, j, :],
-                in0=accs[0],
-                scalar=Q_SCALE,
-                in1=qb_scaled[:].rearrange("p (n d) -> p n d", n=NH),
-                op0=ALU.mult,
-                op1=ALU.add,
-            )
-            nc.scalar.copy(out=o_k[:, :, j, :], in_=accs[1])
-            nc.vector.tensor_tensor(
-                out=o_v[:, :, j, :],
-                in0=accs[2],
-                in1=vb_bc[:].rearrange("p (n d) -> p n d", n=NH),
-                op=ALU.add,
-            )
+            elif i == K:
+                nc.scalar.copy(out=o_sb[:, :, j, :], in_=by_head)
+            else:
+                nc.vector.tensor_tensor(
+                    out=o_sb[:, :, j, :],
+                    in0=by_head,
+                    in1=vb_bc[:].rearrange("p (n d) -> p n d", n=NH),
+                    op=ALU.add,
+                )
 
         def store(b, o_sb, o_dram):
             nc.sync.dma_start(
@@ -163,11 +171,17 @@ def tile_disentangledattention_pa_t_kernel(
         nc.sync.dma_start(out=gb_rows[0:PACK, :], in_=emb_ln_g.rearrange("(t p) -> t p", p=P))
         nc.sync.dma_start(out=gb_rows[PACK : 2 * PACK, :], in_=emb_ln_b.rearrange("(t p) -> t p", p=P))
         load_x(1)
-        w_raw = []
+        w_raw, w_grouped, w_codes, w_scales = [], [], [], []
         for i, w in enumerate((Wq, Wk, Wv)):
             raw = const.tile([P, PACK, H], BF16, name="w_raw%d" % i)
             nc.sync.dma_start(out=raw[:], in_=w.rearrange("(t p) n -> p t n", p=P))
             w_raw.append(raw)
+            g_w = const.tile([P, H, PACK], BF16, name="w_grouped%d" % i, align_bytes=64)
+            w_grouped.append(g_w)
+            codes = const.tile([P, H], U32, name="w_codes%d" % i, align_bytes=64)
+            w_codes.append(codes)
+            scales = const.tile([P, H], U8, name="w_scales%d" % i, align_bytes=64)
+            w_scales.append(scales)
         load_x(2)
         qb_bc = const.tile([P, H], BF16)
         nc.sync.dma_start(out=qb_bc[:], in_=q_bias.partition_broadcast(P))
@@ -184,71 +198,78 @@ def tile_disentangledattention_pa_t_kernel(
         nc.vector.memset(one[:], 1.0)
         warm = const.tile([P, 1], F32)
         nc.scalar.activation(out=warm[:], in_=one[:], func=ACT.Sqrt)
-
-        grouped_w = []
-        for i in range(3):
-            g_w = const.tile([P, H, PACK], BF16, name="grouped_w%d" % i, align_bytes=64)
-            grouped_w.append(g_w)
-        add_pos(nc.vector, 0)
-        add_pos(nc.gpsimd, 1)
-        add_pos(nc.gpsimd, 2)
-        row_stats(0)
-        regroup(nc.scalar.copy, grouped_w[0][:], w_raw[0][:])
-        row_std(0)
         gb_t = psum_acc.tile([P, P], BF16, tag="acc")
         nc.tensor.transpose(gb_t[:], gb_rows[:], ident_bf16[:])
         gb_col = const.tile([P, 2 * PACK], F32)
-        nc.vector.tensor_copy(out=gb_col[:], in_=gb_t[:, 0 : 2 * PACK])
-        row_factors(0)
-        normalise(nc.vector, 0)
-        banks = transpose(0)
-        regroup(nc.scalar.copy, grouped_w[1][:], w_raw[1][:])
-        regroup(nc.scalar.copy, grouped_w[2][:], w_raw[2][:])
-        row_stats(1)
-        row_std(1)
-        row_factors(1)
-        normalise(nc.gpsimd, 1)
-        row_stats(2)
-        w_codes = []
-        w_scales = []
-        for i in range(3):
-            codes = const.tile([P, H], U32, name="w_codes%d" % i, align_bytes=64)
-            scales = const.tile([P, H], U8, name="w_scales%d" % i, align_bytes=64)
-            nc.vector.quantize_mx(
-                out=codes[:].bitcast(FP8X4),
-                scales=scales[:],
-                in_=grouped_w[i][:].rearrange("p n t -> p (n t)"),
-            )
-            w_codes.append(codes)
-            w_scales.append(scales)
         qb_scaled = const.tile([P, H], F32)
-        nc.vector.tensor_scalar_mul(out=qb_scaled[:], in0=qb_bc[:], scalar1=Q_SCALE)
-        for t in range(PACK):
-            gain_bias(0, banks, t)
-        quantise_h(0)
 
-        for b in range(B):
-            if b + 2 < B:
-                row_std(b + 2)
-            if b + 3 < B:
-                add_pos(nc.gpsimd, b + 3)
-            if b + 1 < B:
-                banks = transpose(b + 1)
-            o_q = outs.tile([P, NH, ROW_TILES, HD], F32, name="o_q")
-            o_k = outs.tile([P, NH, ROW_TILES, HD], F32, name="o_k")
-            o_v = outs.tile([P, NH, ROW_TILES, HD], F32, name="o_v")
-            for j in range(ROW_TILES):
-                if b + 1 < B:
-                    gain_bias(b + 1, banks, j)
-                project(b, j, o_q, o_k, o_v)
-                if j == 0 and b + 2 < B:
-                    row_factors(b + 2)
-            if b + 2 < B:
-                normalise(nc.gpsimd, b + 2)
-            store(b, o_q, out_0)
-            store(b, o_k, out_1)
-            store(b, o_v, out_2)
-            if b + 3 < B:
-                row_stats(b + 3)
-            if b + 1 < B:
-                quantise_h(b + 1)
+        for step in range(-4, B):
+            o_sb = []
+            if live(step):
+                for i in range(3):
+                    o_i = outs.tile([P, NH, ROW_TILES, HD], F32, name="o%d" % i)
+                    o_sb.append(o_i)
+            if live(step + 2):
+                normalise(step + 2)
+            if live(step + 4):
+                add_pos(step + 4)
+            if step == -3:
+                regroup(w_grouped[Q][:], w_raw[Q][:])
+
+            if live(step):
+                project(step, Q, 0, o_sb[Q])
+                project(step, Q, 1, o_sb[Q])
+                project(step, K, 0, o_sb[K])
+            if live(step + 1):
+                regroup_h(step + 1)
+            if live(step + 3):
+                row_stats(step + 3, 0)
+                row_stats(step + 3, 1)
+            if live(step):
+                project(step, Q, 2, o_sb[Q])
+                project(step, Q, 3, o_sb[Q])
+                project(step, K, 1, o_sb[K])
+                store(step, o_sb[Q], out_0)
+            if live(step + 2):
+                transpose(step + 2)
+            if live(step + 3):
+                row_stats(step + 3, 2)
+                row_stats(step + 3, 3)
+            if step == -3:
+                nc.vector.tensor_copy(out=gb_col[:], in_=gb_t[:, 0 : 2 * PACK])
+            if live(step + 2):
+                gain_bias(step + 2, 0)
+            if live(step + 3):
+                row_std(step + 3)
+            if step == -3:
+                regroup(w_grouped[K][:], w_raw[K][:])
+                regroup(w_grouped[V][:], w_raw[V][:])
+            if step == -2:
+                for i in range(3):
+                    nc.vector.quantize_mx(
+                        out=w_codes[i][:].bitcast(FP8X4),
+                        scales=w_scales[i][:],
+                        in_=w_grouped[i][:].rearrange("p n t -> p (n t)"),
+                    )
+                nc.vector.tensor_scalar_mul(out=qb_scaled[:], in0=qb_bc[:], scalar1=Q_SCALE)
+            if live(step + 1):
+                quantise_h(step + 1)
+            if live(step + 2):
+                gain_bias(step + 2, 1)
+            if live(step):
+                project(step, V, 0, o_sb[V])
+                project(step, V, 1, o_sb[V])
+                project(step, K, 2, o_sb[K])
+            if live(step + 3):
+                row_factors(step + 3)
+            if live(step + 2):
+                gain_bias(step + 2, 2)
+            if live(step):
+                project(step, V, 2, o_sb[V])
+                project(step, V, 3, o_sb[V])
+                project(step, K, 3, o_sb[K])
+            if live(step + 2):
+                gain_bias(step + 2, 3)
+            if live(step):
+                store(step, o_sb[K], out_1)
+                store(step, o_sb[V], out_2)

@@ -38,7 +38,7 @@ def tile_disentangledattention_pa_t_kernel(
         psum_t = ctx.enter_context(tc.psum_pool(name="psum_t", bufs=1))
         psum_acc = ctx.enter_context(tc.psum_pool(name="psum_acc", bufs=4))
 
-        x_sb, u, stats, mean_var, std, neg_mean, rstd = {}, {}, {}, {}, {}, {}, {}
+        x_sb, u, stats, mean_var, neg_mean, rstd = {}, {}, {}, {}, {}, {}
         z, z_t, h_t, grouped, h_codes, h_scales = {}, {}, {}, {}, {}, {}
 
         def live(b):
@@ -59,7 +59,10 @@ def tile_disentangledattention_pa_t_kernel(
 
         def add_pos(b):
             u[b] = work.tile([P, ROW_TILES, H], F32, name="u", bufs=3)
-            elementwise_engine(b).tensor_tensor(out=u[b][:], in0=x_sb[b][:], in1=pos_sb[:], op=ALU.add)
+            for j in range(ROW_TILES):
+                elementwise_engine(b).tensor_tensor(
+                    out=u[b][:, j, :], in0=x_sb[b][:, j, :], in1=pos_sb[:, j, :], op=ALU.add
+                )
             stats[b] = small.tile([P, ROW_TILES, 6], F32, name="stats")
             mean_var[b] = small.tile([P, ROW_TILES, 2], F32, name="mean_var")
 
@@ -67,17 +70,13 @@ def tile_disentangledattention_pa_t_kernel(
             nc.vector.bn_stats(out=stats[b][:, j, :], in_=u[b][:, j, :])
             nc.vector.bn_aggr(out=mean_var[b][:, j, :], in_=stats[b][:, j, :])
 
-        def row_std(b):
-            std[b] = small.tile([P, ROW_TILES], F32, name="std")
-            nc.scalar.activation(
-                out=std[b][:], in_=mean_var[b][:, :, 1], func=ACT.Sqrt, bias=EPS, scale=1.0
-            )
-
         def row_factors(b):
             rstd[b] = small.tile([P, ROW_TILES], F32, name="rstd")
-            nc.vector.reciprocal(out=rstd[b][:], in_=std[b][:])
+            nc.scalar.activation(
+                out=rstd[b][:], in_=mean_var[b][:, :, 1], func=ACT.Abs_reciprocal_sqrt, bias=EPS, scale=1.0
+            )
             neg_mean[b] = small.tile([P, ROW_TILES], F32, name="neg_mean")
-            nc.vector.tensor_scalar_mul(out=neg_mean[b][:], in0=mean_var[b][:, :, 0], scalar1=-1.0)
+            nc.scalar.mul(out=neg_mean[b][:], in_=mean_var[b][:, :, 0], mul=-1.0)
 
         def normalise(b):
             z[b] = work.tile([P, ROW_TILES, H], F32, name="z")
@@ -197,7 +196,7 @@ def tile_disentangledattention_pa_t_kernel(
         one = const.tile([P, 1], F32)
         nc.vector.memset(one[:], 1.0)
         warm = const.tile([P, 1], F32)
-        nc.scalar.activation(out=warm[:], in_=one[:], func=ACT.Sqrt)
+        nc.scalar.activation(out=warm[:], in_=one[:], func=ACT.Abs_reciprocal_sqrt)
         gb_t = psum_acc.tile([P, P], BF16, tag="acc")
         nc.tensor.transpose(gb_t[:], gb_rows[:], ident_bf16[:])
         gb_col = const.tile([P, 2 * PACK], F32)
@@ -240,7 +239,7 @@ def tile_disentangledattention_pa_t_kernel(
             if live(step + 2):
                 gain_bias(step + 2, 0)
             if live(step + 3):
-                row_std(step + 3)
+                row_factors(step + 3)
             if step == -3:
                 regroup(w_grouped[K][:], w_raw[K][:])
                 regroup(w_grouped[V][:], w_raw[V][:])
@@ -260,8 +259,6 @@ def tile_disentangledattention_pa_t_kernel(
                 project(step, V, 0, o_sb[V])
                 project(step, V, 1, o_sb[V])
                 project(step, K, 2, o_sb[K])
-            if live(step + 3):
-                row_factors(step + 3)
             if live(step + 2):
                 gain_bias(step + 2, 2)
             if live(step):

@@ -38,7 +38,7 @@ def tile_disentangledattention_pa_t_kernel(
         psum_t = ctx.enter_context(tc.psum_pool(name="psum_t", bufs=1))
         psum_acc = ctx.enter_context(tc.psum_pool(name="psum_acc", bufs=4))
 
-        x_sb, u, stats, mean_var, neg_mean, rstd = {}, {}, {}, {}, {}, {}
+        x_sb, u, stats, mean_var, std, neg_mean, rstd = {}, {}, {}, {}, {}, {}, {}
         z, z_t, h_t, grouped, h_codes, h_scales = {}, {}, {}, {}, {}, {}
 
         def live(b):
@@ -59,10 +59,7 @@ def tile_disentangledattention_pa_t_kernel(
 
         def add_pos(b):
             u[b] = work.tile([P, ROW_TILES, H], F32, name="u", bufs=3)
-            for j in range(ROW_TILES):
-                elementwise_engine(b).tensor_tensor(
-                    out=u[b][:, j, :], in0=x_sb[b][:, j, :], in1=pos_sb[:, j, :], op=ALU.add
-                )
+            elementwise_engine(b).tensor_tensor(out=u[b][:], in0=x_sb[b][:], in1=pos_sb[:], op=ALU.add)
             stats[b] = small.tile([P, ROW_TILES, 6], F32, name="stats")
             mean_var[b] = small.tile([P, ROW_TILES, 2], F32, name="mean_var")
 
@@ -70,18 +67,23 @@ def tile_disentangledattention_pa_t_kernel(
             nc.vector.bn_stats(out=stats[b][:, j, :], in_=u[b][:, j, :])
             nc.vector.bn_aggr(out=mean_var[b][:, j, :], in_=stats[b][:, j, :])
 
+        def row_std(b):
+            std[b] = small.tile([P, ROW_TILES], F32, name="std")
+            nc.scalar.activation(
+                out=std[b][:], in_=mean_var[b][:, :, 1], func=ACT.Sqrt, bias=EPS, scale=1.0
+            )
+
         def row_factors(b):
             rstd[b] = small.tile([P, ROW_TILES], F32, name="rstd")
-            nc.scalar.activation(
-                out=rstd[b][:], in_=mean_var[b][:, :, 1], func=ACT.Abs_reciprocal_sqrt, bias=EPS, scale=1.0
-            )
+            nc.vector.reciprocal(out=rstd[b][:], in_=std[b][:])
             neg_mean[b] = small.tile([P, ROW_TILES], F32, name="neg_mean")
-            nc.scalar.mul(out=neg_mean[b][:], in_=mean_var[b][:, :, 0], mul=-1.0)
+            nc.vector.tensor_scalar_mul(out=neg_mean[b][:], in0=mean_var[b][:, :, 0], scalar1=-1.0)
 
         def normalise(b):
             z[b] = work.tile([P, ROW_TILES, H], F32, name="z")
             for j in range(ROW_TILES):
-                elementwise_engine(b).tensor_scalar(
+                engine = elementwise_engine(b) if j % 2 == 0 else nc.vector
+                engine.tensor_scalar(
                     out=z[b][:, j, :],
                     in0=u[b][:, j, :],
                     scalar1=neg_mean[b][:, j : j + 1],
@@ -196,7 +198,7 @@ def tile_disentangledattention_pa_t_kernel(
         one = const.tile([P, 1], F32)
         nc.vector.memset(one[:], 1.0)
         warm = const.tile([P, 1], F32)
-        nc.scalar.activation(out=warm[:], in_=one[:], func=ACT.Abs_reciprocal_sqrt)
+        nc.scalar.activation(out=warm[:], in_=one[:], func=ACT.Sqrt)
         gb_t = psum_acc.tile([P, P], BF16, tag="acc")
         nc.tensor.transpose(gb_t[:], gb_rows[:], ident_bf16[:])
         gb_col = const.tile([P, 2 * PACK], F32)
@@ -239,7 +241,7 @@ def tile_disentangledattention_pa_t_kernel(
             if live(step + 2):
                 gain_bias(step + 2, 0)
             if live(step + 3):
-                row_factors(step + 3)
+                row_std(step + 3)
             if step == -3:
                 regroup(w_grouped[K][:], w_raw[K][:])
                 regroup(w_grouped[V][:], w_raw[V][:])
@@ -259,6 +261,8 @@ def tile_disentangledattention_pa_t_kernel(
                 project(step, V, 0, o_sb[V])
                 project(step, V, 1, o_sb[V])
                 project(step, K, 2, o_sb[K])
+            if live(step + 3):
+                row_factors(step + 3)
             if live(step + 2):
                 gain_bias(step + 2, 2)
             if live(step):

@@ -35,8 +35,8 @@ def tile_disentangledattention_pa_t_kernel(
         work = ctx.enter_context(tc.tile_pool(name="work", bufs=2))
         small = ctx.enter_context(tc.tile_pool(name="small", bufs=3))
         outs = ctx.enter_context(tc.tile_pool(name="outs", bufs=3))
-        psum_t = ctx.enter_context(tc.psum_pool(name="psum_t", bufs=1))
-        psum_acc = ctx.enter_context(tc.psum_pool(name="psum_acc", bufs=4))
+        psum_t = ctx.enter_context(tc.psum_pool(name="psum_t", bufs=3))
+        psum_acc = ctx.enter_context(tc.psum_pool(name="psum_acc", bufs=5))
 
         x_sb, u, stats, mean_var, std, neg_mean, rstd = {}, {}, {}, {}, {}, {}, {}
         z, z_t, h_t, grouped, h_codes, h_scales = {}, {}, {}, {}, {}, {}
@@ -48,8 +48,8 @@ def tile_disentangledattention_pa_t_kernel(
             x_sb[b] = xs.tile([P, ROW_TILES, H], BF16, name="x_b")
             nc.sync.dma_start(out=x_sb[b][:], in_=x[b].rearrange("(p j) h -> p j h", j=ROW_TILES))
 
-        def regroup(dst, src):
-            nc.scalar.copy(
+        def regroup(copy, dst, src):
+            copy(
                 out=dst.rearrange("p (c i) t -> p c t i", i=4),
                 in_=src.rearrange("p t (c i) -> p c t i", i=4),
             )
@@ -81,6 +81,7 @@ def tile_disentangledattention_pa_t_kernel(
 
         def normalise(b):
             z[b] = work.tile([P, ROW_TILES, H], F32, name="z")
+            h_t[b] = work.tile([P, PACK, S], BF16, name="h_t")
             for j in range(ROW_TILES):
                 engine = elementwise_engine(b) if j % 2 == 0 else nc.vector
                 engine.tensor_scalar(
@@ -92,22 +93,17 @@ def tile_disentangledattention_pa_t_kernel(
                     op1=ALU.mult,
                 )
 
-        def transpose(b):
-            z_t[b] = []
-            for t in range(PACK):
-                bank = psum_t.tile([P, S], F32, name="z_t%d" % t)
-                z_t[b].append(bank)
+        def transpose(b, t):
+            z_t[b, t] = psum_t.tile([P, S], F32, name="z_t")
             for j in range(ROW_TILES):
-                for t in range(PACK):
-                    nc.tensor.transpose(
-                        z_t[b][t][:, j * P : (j + 1) * P], z[b][:, j, t * P : (t + 1) * P], ident_f32[:]
-                    )
-            h_t[b] = work.tile([P, PACK, S], BF16, name="h_t")
+                nc.tensor.transpose(
+                    z_t[b, t][:, j * P : (j + 1) * P], z[b][:, j, t * P : (t + 1) * P], ident_f32[:]
+                )
 
         def gain_bias(b, t):
             nc.scalar.activation(
                 out=h_t[b][:, t, :],
-                in_=z_t[b][t][:],
+                in_=z_t[b, t][:],
                 func=ACT.Identity,
                 scale=gb_col[:, t : t + 1],
                 bias=gb_col[:, PACK + t : PACK + t + 1],
@@ -115,7 +111,7 @@ def tile_disentangledattention_pa_t_kernel(
 
         def regroup_h(b):
             grouped[b] = work.tile([P, S, PACK], BF16, name="grouped", align_bytes=64)
-            regroup(grouped[b][:], h_t[b][:])
+            regroup(nc.scalar.copy if b < B - 2 else nc.vector.tensor_copy, grouped[b][:], h_t[b][:])
 
         def quantise_h(b):
             h_codes[b] = work.tile([P, S], U32, name="h_codes", align_bytes=64)
@@ -215,7 +211,7 @@ def tile_disentangledattention_pa_t_kernel(
             if live(step + 4):
                 add_pos(step + 4)
             if step == -3:
-                regroup(w_grouped[Q][:], w_raw[Q][:])
+                regroup(nc.scalar.copy, w_grouped[Q][:], w_raw[Q][:])
 
             if live(step):
                 project(step, Q, 0, o_sb[Q])
@@ -232,7 +228,9 @@ def tile_disentangledattention_pa_t_kernel(
                 project(step, K, 1, o_sb[K])
                 store(step, o_sb[Q], out_0)
             if live(step + 2):
-                transpose(step + 2)
+                transpose(step + 2, 0)
+                transpose(step + 2, 1)
+                transpose(step + 2, 2)
             if live(step + 3):
                 row_stats(step + 3, 2)
                 row_stats(step + 3, 3)
@@ -243,8 +241,8 @@ def tile_disentangledattention_pa_t_kernel(
             if live(step + 3):
                 row_std(step + 3)
             if step == -3:
-                regroup(w_grouped[K][:], w_raw[K][:])
-                regroup(w_grouped[V][:], w_raw[V][:])
+                regroup(nc.scalar.copy, w_grouped[K][:], w_raw[K][:])
+                regroup(nc.scalar.copy, w_grouped[V][:], w_raw[V][:])
             if step == -2:
                 for i in range(3):
                     nc.vector.quantize_mx(
@@ -264,6 +262,7 @@ def tile_disentangledattention_pa_t_kernel(
             if live(step + 3):
                 row_factors(step + 3)
             if live(step + 2):
+                transpose(step + 2, 3)
                 gain_bias(step + 2, 2)
             if live(step):
                 project(step, V, 2, o_sb[V])

from contextlib import ExitStack
import math

import concourse.mybir as mybir
from concourse.masks import make_identity

F32 = mybir.dt.float32
BF16 = mybir.dt.bfloat16
U32 = mybir.dt.uint32
U8 = mybir.dt.uint8
FP8X4 = mybir.dt.float8_e4m3fn_x4
ALU = mybir.AluOpType
ACT = mybir.ActivationFunctionType

P = 128
PACK = 4
B, S, H, NH, HD = 8, 512, 512, 4, 128
ROW_TILES = S // P
EPS = 1e-7
Q_SCALE = 1.0 / math.sqrt(HD)

Q, K, V = 0, 1, 2

FLOPS = 2 * B * S * H * 3 * H


def tile_disentangledattention_pa_t_kernel(
    tc, x, pos_emb, emb_ln_g, emb_ln_b, Wq, Wk, Wv, q_bias, v_bias, out_0, out_1, out_2
):
    nc = tc.nc
    with ExitStack() as ctx:
        ctx.enter_context(tc.manual_schedule())
        const = ctx.enter_context(tc.tile_pool(name="const", bufs=1))
        xs = ctx.enter_context(tc.tile_pool(name="xs", bufs=B))
        work = ctx.enter_context(tc.tile_pool(name="work", bufs=2))
        small = ctx.enter_context(tc.tile_pool(name="small", bufs=3))
        outs = ctx.enter_context(tc.tile_pool(name="outs", bufs=3))
        psum_t = ctx.enter_context(tc.psum_pool(name="psum_t", bufs=3))
        psum_acc = ctx.enter_context(tc.psum_pool(name="psum_acc", bufs=5))

        x_sb, u, stats, mean_var, std, neg_mean, rstd = {}, {}, {}, {}, {}, {}, {}
        z, z_t, h_t, grouped, h_codes, h_scales = {}, {}, {}, {}, {}, {}

        def live(b):
            return 0 <= b < B

        def load_x(b):
            x_sb[b] = xs.tile([P, ROW_TILES, H], BF16, name="x_b")
            nc.sync.dma_start(out=x_sb[b][:], in_=x[b].rearrange("(p j) h -> p j h", j=ROW_TILES))

        def regroup(copy, dst, src):
            copy(
                out=dst.rearrange("p (c i) t -> p c t i", i=4),
                in_=src.rearrange("p t (c i) -> p c t i", i=4),
            )

        def elementwise_engine(b):
            return nc.vector if b == 0 else nc.gpsimd

        def add_pos(b):
            u[b] = work.tile([P, ROW_TILES, H], F32, name="u", bufs=3)
            elementwise_engine(b).tensor_tensor(out=u[b][:], in0=x_sb[b][:], in1=pos_sb[:], op=ALU.add)
            stats[b] = small.tile([P, ROW_TILES, 6], F32, name="stats")
            mean_var[b] = small.tile([P, ROW_TILES, 2], F32, name="mean_var")

        def row_stats(b, j):
            nc.vector.bn_stats(out=stats[b][:, j, :], in_=u[b][:, j, :])
            nc.vector.bn_aggr(out=mean_var[b][:, j, :], in_=stats[b][:, j, :])

        def row_std(b):
            std[b] = small.tile([P, ROW_TILES], F32, name="std")
            nc.scalar.activation(
                out=std[b][:], in_=mean_var[b][:, :, 1], func=ACT.Sqrt, bias=EPS, scale=1.0
            )

        def row_factors(b):
            rstd[b] = small.tile([P, ROW_TILES], F32, name="rstd")
            nc.vector.reciprocal(out=rstd[b][:], in_=std[b][:])
            neg_mean[b] = small.tile([P, ROW_TILES], F32, name="neg_mean")
            nc.vector.tensor_scalar_mul(out=neg_mean[b][:], in0=mean_var[b][:, :, 0], scalar1=-1.0)

        def normalise(b):
            z[b] = work.tile([P, ROW_TILES, H], F32, name="z")
            h_t[b] = work.tile([P, PACK, S], BF16, name="h_t")
            for j in range(ROW_TILES):
                engine = elementwise_engine(b) if j % 2 == 0 else nc.vector
                engine.tensor_scalar(
                    out=z[b][:, j, :],
                    in0=u[b][:, j, :],
                    scalar1=neg_mean[b][:, j : j + 1],
                    scalar2=rstd[b][:, j : j + 1],
                    op0=ALU.add,
                    op1=ALU.mult,
                )

        def transpose(b, t):
            z_t[b, t] = psum_t.tile([P, S], F32, name="z_t")
            for j in range(ROW_TILES):
                nc.tensor.transpose(
                    z_t[b, t][:, j * P : (j + 1) * P], z[b][:, j, t * P : (t + 1) * P], ident_f32[:]
                )

        def gain_bias(b, t):
            nc.scalar.activation(
                out=h_t[b][:, t, :],
                in_=z_t[b, t][:],
                func=ACT.Identity,
                scale=gb_col[:, t : t + 1],
                bias=gb_col[:, PACK + t : PACK + t + 1],
            )

        def regroup_h(b):
            grouped[b] = work.tile([P, S, PACK], BF16, name="grouped", align_bytes=64)
            regroup(nc.scalar.copy if b < B - 2 else nc.vector.tensor_copy, grouped[b][:], h_t[b][:])

        def quantise_h(b):
            h_codes[b] = work.tile([P, S], U32, name="h_codes", align_bytes=64)
            h_scales[b] = work.tile([P, S], U8, name="h_scales", align_bytes=64)
            nc.vector.quantize_mx(
                out=h_codes[b][:].bitcast(FP8X4),
                scales=h_scales[b][:],
                in_=grouped[b][:].rearrange("p r t -> p (r t)"),
            )

        def project(b, i, j, o_sb):
            rows = slice(j * P, (j + 1) * P)
            acc = psum_acc.tile([P, H], F32, name="acc", tag="acc")
            nc.tensor.matmul_mx(
                out=acc[:],
                lhsT=h_codes[b][:, rows].bitcast(FP8X4),
                lhsT_scale=h_scales[b][:, rows],
                rhs=w_codes[i][:].bitcast(FP8X4),
                rhs_scale=w_scales[i][:],
                start=True,
                stop=True,
            )
            by_head = acc[:].rearrange("p (n d) -> p n d", n=NH)
            if i == Q:
                nc.vector.scalar_tensor_tensor(
                    out=o_sb[:, :, j, :],
                    in0=by_head,
                    scalar=Q_SCALE,
                    in1=qb_scaled[:].rearrange("p (n d) -> p n d", n=NH),
                    op0=ALU.mult,
                    op1=ALU.add,
                )
            elif i == K:
                nc.scalar.copy(out=o_sb[:, :, j, :], in_=by_head)
            else:
                nc.vector.tensor_tensor(
                    out=o_sb[:, :, j, :],
                    in0=by_head,
                    in1=vb_bc[:].rearrange("p (n d) -> p n d", n=NH),
                    op=ALU.add,
                )

        def store(b, o_sb, o_dram):
            nc.sync.dma_start(
                out=o_dram[b].rearrange("n (p j) d -> p n (j d)", j=ROW_TILES),
                in_=o_sb[:].rearrange("p n j d -> p n (j d)"),
            )

        load_x(0)
        pos_sb = const.tile([P, ROW_TILES, H], BF16)
        nc.sync.dma_start(out=pos_sb[:], in_=pos_emb.rearrange("(p j) h -> p j h", j=ROW_TILES))
        gb_rows = const.tile([P, P], BF16)
        nc.vector.memset(gb_rows[:], 0.0)
        nc.sync.dma_start(out=gb_rows[0:PACK, :], in_=emb_ln_g.rearrange("(t p) -> t p", p=P))
        nc.sync.dma_start(out=gb_rows[PACK : 2 * PACK, :], in_=emb_ln_b.rearrange("(t p) -> t p", p=P))
        load_x(1)
        w_raw, w_grouped, w_codes, w_scales = [], [], [], []
        for i, w in enumerate((Wq, Wk, Wv)):
            raw = const.tile([P, PACK, H], BF16, name="w_raw%d" % i)
            nc.sync.dma_start(out=raw[:], in_=w.rearrange("(t p) n -> p t n", p=P))
            w_raw.append(raw)
            g_w = const.tile([P, H, PACK], BF16, name="w_grouped%d" % i, align_bytes=64)
            w_grouped.append(g_w)
            codes = const.tile([P, H], U32, name="w_codes%d" % i, align_bytes=64)
            w_codes.append(codes)
            scales = const.tile([P, H], U8, name="w_scales%d" % i, align_bytes=64)
            w_scales.append(scales)
        load_x(2)
        qb_bc = const.tile([P, H], BF16)
        nc.sync.dma_start(out=qb_bc[:], in_=q_bias.partition_broadcast(P))
        vb_bc = const.tile([P, H], BF16)
        nc.sync.dma_start(out=vb_bc[:], in_=v_bias.partition_broadcast(P))
        for b in range(3, B):
            load_x(b)

        ident_f32 = const.tile([P, P], F32)
        make_identity(nc, ident_f32[:])
        ident_bf16 = const.tile([P, P], BF16)
        make_identity(nc, ident_bf16[:])
        one = const.tile([P, 1], F32)
        nc.vector.memset(one[:], 1.0)
        warm = const.tile([P, 1], F32)
        nc.scalar.activation(out=warm[:], in_=one[:], func=ACT.Sqrt)
        gb_t = psum_acc.tile([P, P], BF16, tag="acc")
        nc.tensor.transpose(gb_t[:], gb_rows[:], ident_bf16[:])
        gb_col = const.tile([P, 2 * PACK], F32)
        qb_scaled = const.tile([P, H], F32)

        for step in range(-4, B):
            o_sb = []
            if live(step):
                for i in range(3):
                    o_i = outs.tile([P, NH, ROW_TILES, HD], F32, name="o%d" % i)
                    o_sb.append(o_i)
            if live(step + 2):
                normalise(step + 2)
            if live(step + 4):
                add_pos(step + 4)
            if step == -3:
                regroup(nc.scalar.copy, w_grouped[Q][:], w_raw[Q][:])

            if live(step):
                project(step, Q, 0, o_sb[Q])
                project(step, Q, 1, o_sb[Q])
                project(step, K, 0, o_sb[K])
            if live(step + 1):
                regroup_h(step + 1)
            if live(step + 3):
                row_stats(step + 3, 0)
                row_stats(step + 3, 1)
            if live(step):
                project(step, Q, 2, o_sb[Q])
                project(step, Q, 3, o_sb[Q])
                project(step, K, 1, o_sb[K])
                store(step, o_sb[Q], out_0)
            if live(step + 2):
                transpose(step + 2, 0)
                transpose(step + 2, 1)
                transpose(step + 2, 2)
            if live(step + 3):
                row_stats(step + 3, 2)
                row_stats(step + 3, 3)
            if step == -3:
                nc.vector.tensor_copy(out=gb_col[:], in_=gb_t[:, 0 : 2 * PACK])
            if live(step + 2):
                gain_bias(step + 2, 0)
            if live(step + 3):
                row_std(step + 3)
            if step == -3:
                regroup(nc.scalar.copy, w_grouped[K][:], w_raw[K][:])
                regroup(nc.scalar.copy, w_grouped[V][:], w_raw[V][:])
            if step == -2:
                for i in range(3):
                    nc.vector.quantize_mx(
                        out=w_codes[i][:].bitcast(FP8X4),
                        scales=w_scales[i][:],
                        in_=w_grouped[i][:].rearrange("p n t -> p (n t)"),
                    )
                nc.vector.tensor_scalar_mul(out=qb_scaled[:], in0=qb_bc[:], scalar1=Q_SCALE)
            if live(step + 1):
                quantise_h(step + 1)
            if live(step + 2):
                gain_bias(step + 2, 1)
            if live(step):
                project(step, V, 0, o_sb[V])
                project(step, V, 1, o_sb[V])
                project(step, K, 2, o_sb[K])
            if live(step + 3):
                row_factors(step + 3)
            if live(step + 2):
                transpose(step + 2, 3)
                gain_bias(step + 2, 2)
            if live(step):
                project(step, V, 2, o_sb[V])
                project(step, V, 3, o_sb[V])
                project(step, K, 3, o_sb[K])
            if live(step + 2):
                gain_bias(step + 2, 3)
            if live(step):
                store(step, o_sb[K], out_1)
                store(step, o_sb[V], out_2)
